import numpy as np
import ml_dtypes


def mxq(x, axis, fmt="e4m3"):
    dtype, down = {"e4m3": (ml_dtypes.float8_e4m3fn, 7), "e5m2": (ml_dtypes.float8_e5m2, 14)}[fmt]
    v = np.moveaxis(np.asarray(x, np.float32).astype(ml_dtypes.bfloat16).astype(np.float64), axis, -1)
    blocks = v.reshape(v.shape[:-1] + (-1, 32))
    amax = np.abs(blocks).max(-1, keepdims=True)
    byte = np.maximum(np.where(amax > 0, np.frexp(amax)[1] - 1 + 127, 0) - down, 1)
    scale = np.exp2(byte - 127.0)
    codes = (blocks / scale).astype(np.float32).astype(dtype).astype(np.float64)
    return np.moveaxis((codes * scale).reshape(v.shape), -1, axis)


WIDE = False


def mx_kscale(k):
    if not WIDE:
        return np.ones(k)
    levels = np.array([10, -10, 5, -5, 0])
    if k % 512:
        return np.exp2(np.random.permutation(np.resize(levels, k // 32))).repeat(32)
    a = np.empty((k // 512, 16))
    for p in range(k // 512):
        a[p, :8] = np.random.permutation(np.resize(levels, 8))
        for g in range(8):
            far = levels[np.abs(levels - a[p, g]) >= 10]
            a[p, g + 8] = far[np.random.randint(len(far))]
    return np.exp2(a.ravel()).repeat(32)


BF16 = ml_dtypes.bfloat16


def bf(x):
    return np.asarray(x, np.float32).astype(BF16)


def f64(x):
    return np.asarray(x).astype(np.float64)


B, T, C, H, D, R = 1, 1024, 2048, 16, 128, 512
EPS = 1e-6
THETA = 10000.0


def rmsnorm(v, w):
    var = np.mean(v * v, axis=-1, keepdims=True)
    return v * (1.0 / np.sqrt(var + EPS)) * w


def rope(v, cos, sin):
    re, im = v[..., 0::2], v[..., 1::2]
    c, s = cos[None, :, None, :], sin[None, :, None, :]
    return np.stack([re * c - im * s, re * s + im * c], axis=-1).reshape(v.shape)


def setup_inputs():
    s = mx_kscale(C)
    ang = np.outer(np.arange(T), 1.0 / THETA ** (np.arange(0, D, 2) / D))
    return {"x": bf(np.random.standard_normal((B, T, C)) * s),
            "wq": bf(np.random.standard_normal((H * D, C)) / np.sqrt(C) / s[None, :]),
            "q_norm_w": bf(1.0 + 0.1 * np.random.standard_normal(D)),
            "freqs_cos": bf(np.cos(ang)), "freqs_sin": bf(np.sin(ang))}


def reference(x, wq, q_norm_w, freqs_cos, freqs_sin):
    xq = (mxq(f64(x), 2, "e4m3") @ mxq(f64(wq), 1, "e4m3").T).reshape(B, T, H, D)
    return rope(rmsnorm(xq, f64(q_norm_w)), f64(freqs_cos), f64(freqs_sin))

@@ -1,0 +1,237 @@
+from contextlib import ExitStack
+
+import concourse.mybir as mybir
+from concourse.masks import make_identity
+
+FP8X4 = mybir.dt.float8_e4m3fn_x4
+BF16 = mybir.dt.bfloat16
+F32 = mybir.dt.float32
+U32 = mybir.dt.uint32
+U8 = mybir.dt.uint8
+ACT = mybir.ActivationFunctionType
+ALU = mybir.AluOpType
+
+P = 128
+TOKENS = 1024
+K = 2048
+HEADS = 16
+HEAD_DIM = 128
+PAIRS = HEAD_DIM // 2
+EPS = 1e-6
+
+K_PASS = 4 * P
+PASSES = K // K_PASS
+PASS_WORDS = K_PASS // 2
+TOKEN_TILES = TOKENS // P
+BLOCK_HEADS = 4
+BLOCK_COLS = BLOCK_HEADS * HEAD_DIM
+BLOCKS = HEADS // BLOCK_HEADS
+GROUPS = BLOCKS * TOKEN_TILES
+UNIT_COLS = 512
+
+W_LEAD = 5
+X_LEAD = 2
+LOAD_LEAD = 8
+
+FLOPS = 2 * TOKENS * K * HEADS * HEAD_DIM
+
+
+def tile_mla_pb_kernel(tc, x, wq, q_norm_w, freqs_cos, freqs_sin, out):
+    nc = tc.nc
+    x_view = x.rearrange("b (p t) k -> p (b t) k", t=TOKEN_TILES)
+    cos_view = freqs_cos.rearrange("(p t) j -> p t j", t=TOKEN_TILES)
+    sin_view = freqs_sin.rearrange("(p t) j -> p t j", t=TOKEN_TILES)
+    out_view = out.rearrange("b (p t) h d -> p (b t) (h d)", t=TOKEN_TILES)
+    wq_view = wq.rearrange("(h p) k -> p h k", p=P)
+
+    with ExitStack() as ctx:
+        const = ctx.enter_context(tc.tile_pool(name="const", bufs=1))
+        raw = ctx.enter_context(tc.tile_pool(name="raw", bufs=1))
+        keep = ctx.enter_context(tc.tile_pool(name="keep", bufs=1))
+        stage = ctx.enter_context(tc.tile_pool(name="stage", bufs=4))
+        work = ctx.enter_context(tc.tile_pool(name="work", bufs=3))
+        result = ctx.enter_context(tc.tile_pool(name="result", bufs=6))
+        small = ctx.enter_context(tc.tile_pool(name="small", bufs=4))
+        tpsum = ctx.enter_context(tc.psum_pool(name="tpsum", bufs=4))
+        mpsum = ctx.enter_context(tc.psum_pool(name="mpsum", bufs=4))
+        ctx.enter_context(tc.manual_schedule())
+
+        x_raw = [raw.tile([P, K], BF16, name="x_raw%d" % t) for t in range(TOKEN_TILES)]
+        w_raw = [raw.tile([P, BLOCK_HEADS, K_PASS], BF16, name="w_raw%d" % i) for i in range(BLOCKS * PASSES)]
+
+        cos_sb = const.tile([P, TOKEN_TILES, PAIRS], BF16, name="cos_sb")
+        sin_sb = const.tile([P, TOKEN_TILES, PAIRS], BF16, name="sin_sb")
+        gain_rows = const.tile([P, HEAD_DIM], BF16, name="gain_rows")
+        nc.vector.memset(gain_rows[:], 0.0)
+        nc.scalar.dma_start(out=gain_rows[0:1, :], in_=q_norm_w.unsqueeze(0))
+        nc.scalar.dma_start(out=cos_sb[:], in_=cos_view)
+        nc.scalar.dma_start(out=sin_sb[:], in_=sin_view)
+
+        ident = const.tile([P, P], F32, name="ident")
+        make_identity(nc, ident[:])
+        split_pairs = const.tile([P, P], F32, name="split_pairs")
+        nc.vector.tensor_copy(
+            out=split_pairs[:].rearrange("p (e j) -> p e j", e=2), in_=ident[:].rearrange("p (j e) -> p e j", e=2)
+        )
+        eps_sb = const.tile([P, 1], F32, name="eps_sb")
+        nc.vector.memset(eps_sb[:], EPS)
+        warm = const.tile([P, 1], F32, name="warm")
+        nc.scalar.activation(out=warm[:], in_=eps_sb[:], func=ACT.Abs_reciprocal_sqrt)
+
+        ones = const.tile([P, P], BF16, name="ones")
+        nc.vector.memset(ones[:], 1.0)
+
+        table = const.tile([P, TOKEN_TILES, 2, PAIRS, 2], F32, name="table")
+
+        def build_table():
+            gain_ps = tpsum.tile([P, PAIRS, 2], F32, name="gain_ps", tag="bank")
+            nc.tensor.matmul(
+                out=gain_ps[:].rearrange("p j e -> p (j e)"), lhsT=ones[:], rhs=gain_rows[:], start=True, stop=True
+            )
+            gain_sb = const.tile([P, PAIRS, 2], F32, name="gain_sb")
+            minus_gain = const.tile([P, PAIRS, 2], F32, name="minus_gain")
+            nc.scalar.copy(out=gain_sb[:], in_=gain_ps[:])
+            nc.scalar.mul(out=minus_gain[:], in_=gain_ps[:], mul=-1.0)
+            table_shape = [P, TOKEN_TILES, PAIRS]
+            gain_even = gain_sb[:, :, 0].unsqueeze(1).to_broadcast(table_shape)
+            gain_odd = gain_sb[:, :, 1].unsqueeze(1).to_broadcast(table_shape)
+            minus_gain_odd = minus_gain[:, :, 1].unsqueeze(1).to_broadcast(table_shape)
+            nc.gpsimd.tensor_tensor(out=table[:, :, 0, :, 0], in0=cos_sb[:], in1=gain_even, op=ALU.mult)
+            nc.gpsimd.tensor_tensor(out=table[:, :, 0, :, 1], in0=sin_sb[:], in1=gain_even, op=ALU.mult)
+            nc.gpsimd.tensor_tensor(out=table[:, :, 1, :, 0], in0=sin_sb[:], in1=minus_gain_odd, op=ALU.mult)
+            nc.gpsimd.tensor_tensor(out=table[:, :, 1, :, 1], in0=cos_sb[:], in1=gain_odd, op=ALU.mult)
+
+        x_codes = [keep.tile([P, UNIT_COLS], U32, name="x_codes%d" % t, align_bytes=64) for t in range(TOKEN_TILES)]
+        x_scales = [keep.tile([P, UNIT_COLS], U8, name="x_scales%d" % t, align_bytes=64) for t in range(TOKEN_TILES)]
+        w_codes = [keep.tile([P, UNIT_COLS], U32, name="w_codes%d" % i, align_bytes=64) for i in range(BLOCKS * PASSES)]
+        w_scales = [keep.tile([P, UNIT_COLS], U8, name="w_scales%d" % i, align_bytes=64) for i in range(BLOCKS * PASSES)]
+
+        def x_unit(t):
+            words = x_raw[t][:].bitcast(F32)
+            sources = [words[:, g * PASS_WORDS : (g + 1) * PASS_WORDS] for g in range(PASSES)]
+            return x_view[:, t, :], x_raw[t], sources, x_codes[t], x_scales[t], ident
+
+        def w_unit(b, g):
+            i = b * PASSES + g
+            rows = wq_view[:, b * BLOCK_HEADS : (b + 1) * BLOCK_HEADS, g * K_PASS : (g + 1) * K_PASS]
+            sources = [w_raw[i][:, a, :].bitcast(F32) for a in range(BLOCK_HEADS)]
+            return rows, w_raw[i], sources, w_codes[i], w_scales[i], split_pairs
+
+        def units_of_slot(s):
+            units = []
+            block, g = divmod(s + W_LEAD, TOKEN_TILES)
+            if block < BLOCKS and g < PASSES:
+                units.append(w_unit(block, g))
+            if 0 <= s + X_LEAD < TOKEN_TILES:
+                units.append(x_unit(s + X_LEAD))
+            return units
+
+        def load(unit):
+            nc.sync.dma_start(out=unit[1][:], in_=unit[0])
+
+        def transpose_and_copy(unit):
+            sources = unit[2]
+            grouped = stage.tile([P, 4 * UNIT_COLS], BF16, name="grouped", align_bytes=64)
+            grouped_words = grouped[:].bitcast(F32).rearrange("p (b a r u) -> p b a r u", b=2, a=2, u=2)
+            for b in range(2):
+                bank = tpsum.tile([P, 2, 2, P], F32, name="bank")
+                for a in range(2):
+                    for u in range(2):
+                        nc.tensor.transpose(bank[:, a, u, :], sources[2 * b + a][:, u::2], unit[5][:])
+                nc.scalar.copy(out=grouped_words[:, b], in_=bank[:].rearrange("p a u r -> p a r u"))
+            return grouped
+
+        def quantise(unit, grouped):
+            nc.vector.quantize_mx(out=unit[3][:].bitcast(FP8X4), scales=unit[4][:], in_=grouped[:])
+
+        accs = {}
+        squares_of = {}
+        sumsq_of = {}
+        inv_of = {}
+
+        def multiply(i):
+            b, t = divmod(i, TOKEN_TILES)
+            acc = mpsum.tile([P, BLOCK_COLS], F32, name="acc")
+            for g in range(PASSES):
+                tokens = slice(g * P, (g + 1) * P)
+                nc.tensor.matmul_mx(
+                    out=acc[:],
+                    lhsT=x_codes[t][:, tokens].bitcast(FP8X4),
+                    lhsT_scale=x_scales[t][:, tokens],
+                    rhs=w_codes[b * PASSES + g][:].bitcast(FP8X4),
+                    rhs_scale=w_scales[b * PASSES + g][:],
+                    start=(g == 0),
+                    stop=(g == PASSES - 1),
+                )
+            accs[i] = acc
+
+        def sum_squares(i, heads):
+            if i not in sumsq_of:
+                squares_of[i] = work.tile([P, BLOCK_COLS], F32, name="squares")
+                sumsq_of[i] = small.tile([P, BLOCK_HEADS], F32, name="sumsq")
+            for h in heads:
+                cols = slice(h * HEAD_DIM, (h + 1) * HEAD_DIM)
+                nc.scalar.activation(
+                    out=squares_of[i][:, cols],
+                    in_=accs[i][:, cols],
+                    func=ACT.Square,
+                    accum_out=sumsq_of[i][:, h : h + 1],
+                )
+
+        def inverse_rms(i):
+            inv = small.tile([P, BLOCK_HEADS], F32, name="inv")
+            nc.scalar.activation(
+                out=inv[:], in_=sumsq_of[i][:], func=ACT.Abs_reciprocal_sqrt, bias=eps_sb[:], scale=1.0 / HEAD_DIM
+            )
+            inv_of[i] = inv
+
+        def rotate_and_store(i):
+            b, t = divmod(i, TOKEN_TILES)
+            acc = accs[i]
+            inv = inv_of[i]
+            products = work.tile([P, BLOCK_HEADS, 2, PAIRS, 2], F32, name="products")
+            for h in range(BLOCK_HEADS):
+                nc.vector.scalar_tensor_tensor(
+                    out=products[:, h].rearrange("p x j e -> p (x j) e"),
+                    in0=acc[:, h * HEAD_DIM : (h + 1) * HEAD_DIM].unsqueeze(2).to_broadcast([P, HEAD_DIM, 2]),
+                    scalar=inv[:, h : h + 1],
+                    in1=table[:, t].rearrange("p x j e -> p (x j) e"),
+                    op0=ALU.mult,
+                    op1=ALU.mult,
+                )
+            rotated = result.tile([P, BLOCK_HEADS, HEAD_DIM], F32, name="rotated")
+            adder = nc.vector if i == GROUPS - 1 else nc.gpsimd
+            adder.tensor_tensor(
+                out=rotated[:],
+                in0=products[:, :, 0].rearrange("p h j e -> p h (j e)"),
+                in1=products[:, :, 1].rearrange("p h j e -> p h (j e)"),
+                op=ALU.add,
+            )
+            nc.sync.dma_start(
+                out=out_view[:, t, b * BLOCK_COLS : (b + 1) * BLOCK_COLS],
+                in_=rotated[:].rearrange("p h d -> p (h d)"),
+            )
+
+        first_slot = -W_LEAD
+        for s in range(first_slot, first_slot + LOAD_LEAD):
+            for unit in units_of_slot(s):
+                load(unit)
+        copied = []
+        for s in range(first_slot, GROUPS + 2):
+            for unit in units_of_slot(s + LOAD_LEAD):
+                load(unit)
+            for unit, grouped in copied:
+                quantise(unit, grouped)
+            if 0 <= s - 1 < GROUPS:
+                sum_squares(s - 1, range(0, 1))
+            if 0 <= s - 2 < GROUPS:
+                inverse_rms(s - 2)
+            if 0 <= s - 1 < GROUPS:
+                sum_squares(s - 1, range(1, BLOCK_HEADS))
+            copied = [(unit, transpose_and_copy(unit)) for unit in units_of_slot(s)]
+            if s == first_slot + 1:
+                build_table()
+            if 0 <= s < GROUPS:
+                multiply(s)
+            if 0 <= s - 2 < GROUPS:
+                rotate_and_store(s - 2)

@@ -29,9 +29,9 @@ BLOCKS = HEADS // BLOCK_HEADS
 GROUPS = BLOCKS * TOKEN_TILES
 UNIT_COLS = 512
 
-W_LEAD = 5
-X_LEAD = 2
 LOAD_LEAD = 8
+
+RUNS = [(7, 1), (2, 2), (2, 2), (2, 1), (2, 1), (2, 3), (2, 4), (2, 4), (2, 4), (1, 10)]
 
 FLOPS = 2 * TOKENS * K * HEADS * HEAD_DIM
 
@@ -116,15 +116,6 @@ def tile_mla_pb_kernel(tc, x, wq, q_norm_w, freqs_cos, freqs_sin, out):
             rows = wq_view[:, b * BLOCK_HEADS : (b + 1) * BLOCK_HEADS, g * K_PASS : (g + 1) * K_PASS]
             sources = [w_raw[i][:, a, :].bitcast(F32) for a in range(BLOCK_HEADS)]
             return rows, w_raw[i], sources, w_codes[i], w_scales[i], split_pairs
-
-        def units_of_slot(s):
-            units = []
-            block, g = divmod(s + W_LEAD, TOKEN_TILES)
-            if block < BLOCKS and g < PASSES:
-                units.append(w_unit(block, g))
-            if 0 <= s + X_LEAD < TOKEN_TILES:
-                units.append(x_unit(s + X_LEAD))
-            return units
 
         def load(unit):
             nc.sync.dma_start(out=unit[1][:], in_=unit[0])
@@ -212,26 +203,30 @@ def tile_mla_pb_kernel(tc, x, wq, q_norm_w, freqs_cos, freqs_sin, out):
                 in_=rotated[:].rearrange("p h d -> p (h d)"),
             )
 
-        first_slot = -W_LEAD
-        for s in range(first_slot, first_slot + LOAD_LEAD):
-            for unit in units_of_slot(s):
-                load(unit)
-        copied = []
-        for s in range(first_slot, GROUPS + 2):
-            for unit in units_of_slot(s + LOAD_LEAD):
-                load(unit)
-            for unit, grouped in copied:
-                quantise(unit, grouped)
-            if 0 <= s - 1 < GROUPS:
-                sum_squares(s - 1, range(0, 1))
-            if 0 <= s - 2 < GROUPS:
-                inverse_rms(s - 2)
-            if 0 <= s - 1 < GROUPS:
-                sum_squares(s - 1, range(1, BLOCK_HEADS))
-            copied = [(unit, transpose_and_copy(unit)) for unit in units_of_slot(s)]
-            if s == first_slot + 1:
-                build_table()
-            if 0 <= s < GROUPS:
-                multiply(s)
-            if 0 <= s - 2 < GROUPS:
-                rotate_and_store(s - 2)
+        units = [w_unit(0, g) for g in range(PASSES)] + [x_unit(t) for t in range(TOKEN_TILES)]
+        units += [w_unit(b, g) for b in range(1, BLOCKS) for g in range(PASSES)]
+        for unit in units[:LOAD_LEAD]:
+            load(unit)
+        done_units = 0
+        done_groups = 0
+        for run_units, run_groups in RUNS:
+            run = units[done_units : done_units + run_units]
+            for n, unit in enumerate(run):
+                if done_units + n + LOAD_LEAD < len(units):
+                    load(units[done_units + n + LOAD_LEAD])
+                quantise(unit, transpose_and_copy(unit))
+                if done_units + n == 1:
+                    build_table()
+            done_units += run_units
+            for n in range(run_groups):
+                i = done_groups + n
+                multiply(i)
+                sum_squares(i, range(0, 1))
+                if n > 0:
+                    inverse_rms(i - 1)
+                    rotate_and_store(i - 1)
+                sum_squares(i, range(1, BLOCK_HEADS))
+            if run_groups:
+                inverse_rms(done_groups + run_groups - 1)
+                rotate_and_store(done_groups + run_groups - 1)
+            done_groups += run_groups

@@ -26,12 +26,11 @@ TOKEN_TILES = TOKENS // P
 BLOCK_HEADS = 4
 BLOCK_COLS = BLOCK_HEADS * HEAD_DIM
 BLOCKS = HEADS // BLOCK_HEADS
-GROUPS = BLOCKS * TOKEN_TILES
-UNIT_COLS = 512
 
 LOAD_LEAD = 8
+TABLE_UNIT = 1
 
-RUNS = [(7, 1), (2, 2), (2, 2), (2, 1), (2, 1), (2, 3), (2, 4), (2, 4), (2, 4), (1, 10)]
+RUNS = [(5, 0), (2, 2), (2, 2), (2, 2), (2, 1), (2, 1), (2, 3), (2, 3), (2, 4), (2, 4), (1, 12)]
 
 FLOPS = 2 * TOKENS * K * HEADS * HEAD_DIM
 
@@ -56,16 +55,33 @@ def tile_mla_pb_kernel(tc, x, wq, q_norm_w, freqs_cos, freqs_sin, out):
         mpsum = ctx.enter_context(tc.psum_pool(name="mpsum", bufs=4))
         ctx.enter_context(tc.manual_schedule())
 
+        x_codes = [keep.tile([P, K // 4], U32, name="x_codes%d" % t, align_bytes=64) for t in range(TOKEN_TILES)]
+        x_scales = [keep.tile([P, K // 4], U8, name="x_scales%d" % t, align_bytes=64) for t in range(TOKEN_TILES)]
+        w_codes = [keep.tile([P, BLOCK_COLS], U32, name="w_codes%d" % i, align_bytes=64) for i in range(BLOCKS * PASSES)]
+        w_scales = [keep.tile([P, BLOCK_COLS], U8, name="w_scales%d" % i, align_bytes=64) for i in range(BLOCKS * PASSES)]
+
         x_raw = [raw.tile([P, K], BF16, name="x_raw%d" % t) for t in range(TOKEN_TILES)]
-        w_raw = [raw.tile([P, BLOCK_HEADS, K_PASS], BF16, name="w_raw%d" % i) for i in range(BLOCKS * PASSES)]
+        w_raw = [raw.tile([P, K], BF16, name="w_raw%d" % h) for h in range(HEADS)]
+        units = [("x", 0)] + [("w", h) for h in range(BLOCK_HEADS)]
+        units += [("x", t) for t in range(1, TOKEN_TILES)] + [("w", h) for h in range(BLOCK_HEADS, HEADS)]
+
+        def load(unit):
+            kind, n = unit
+            if kind == "x":
+                nc.sync.dma_start(out=x_raw[n][:], in_=x_view[:, n, :])
+            else:
+                nc.sync.dma_start(out=w_raw[n][:], in_=wq_view[:, n, :])
 
         cos_sb = const.tile([P, TOKEN_TILES, PAIRS], BF16, name="cos_sb")
         sin_sb = const.tile([P, TOKEN_TILES, PAIRS], BF16, name="sin_sb")
         gain_rows = const.tile([P, HEAD_DIM], BF16, name="gain_rows")
         nc.vector.memset(gain_rows[:], 0.0)
         nc.scalar.dma_start(out=gain_rows[0:1, :], in_=q_norm_w.unsqueeze(0))
-        nc.scalar.dma_start(out=cos_sb[:], in_=cos_view)
-        nc.scalar.dma_start(out=sin_sb[:], in_=sin_view)
+        load(units[0])
+        nc.sync.dma_start(out=cos_sb[:], in_=cos_view)
+        nc.sync.dma_start(out=sin_sb[:], in_=sin_view)
+        for unit in units[1:LOAD_LEAD]:
+            load(unit)
 
         ident = const.tile([P, P], F32, name="ident")
         make_identity(nc, ident[:])
@@ -92,75 +108,77 @@ def tile_mla_pb_kernel(tc, x, wq, q_norm_w, freqs_cos, freqs_sin, out):
             minus_gain = const.tile([P, PAIRS, 2], F32, name="minus_gain")
             nc.scalar.copy(out=gain_sb[:], in_=gain_ps[:])
             nc.scalar.mul(out=minus_gain[:], in_=gain_ps[:], mul=-1.0)
-            table_shape = [P, TOKEN_TILES, PAIRS]
-            gain_even = gain_sb[:, :, 0].unsqueeze(1).to_broadcast(table_shape)
-            gain_odd = gain_sb[:, :, 1].unsqueeze(1).to_broadcast(table_shape)
-            minus_gain_odd = minus_gain[:, :, 1].unsqueeze(1).to_broadcast(table_shape)
-            nc.gpsimd.tensor_tensor(out=table[:, :, 0, :, 0], in0=cos_sb[:], in1=gain_even, op=ALU.mult)
-            nc.gpsimd.tensor_tensor(out=table[:, :, 0, :, 1], in0=sin_sb[:], in1=gain_even, op=ALU.mult)
-            nc.gpsimd.tensor_tensor(out=table[:, :, 1, :, 0], in0=sin_sb[:], in1=minus_gain_odd, op=ALU.mult)
-            nc.gpsimd.tensor_tensor(out=table[:, :, 1, :, 1], in0=cos_sb[:], in1=gain_odd, op=ALU.mult)
-
-        x_codes = [keep.tile([P, UNIT_COLS], U32, name="x_codes%d" % t, align_bytes=64) for t in range(TOKEN_TILES)]
-        x_scales = [keep.tile([P, UNIT_COLS], U8, name="x_scales%d" % t, align_bytes=64) for t in range(TOKEN_TILES)]
-        w_codes = [keep.tile([P, UNIT_COLS], U32, name="w_codes%d" % i, align_bytes=64) for i in range(BLOCKS * PASSES)]
-        w_scales = [keep.tile([P, UNIT_COLS], U8, name="w_scales%d" % i, align_bytes=64) for i in range(BLOCKS * PASSES)]
-
-        def x_unit(t):
-            words = x_raw[t][:].bitcast(F32)
-            sources = [words[:, g * PASS_WORDS : (g + 1) * PASS_WORDS] for g in range(PASSES)]
-            return x_view[:, t, :], x_raw[t], sources, x_codes[t], x_scales[t], ident
-
-        def w_unit(b, g):
-            i = b * PASSES + g
-            rows = wq_view[:, b * BLOCK_HEADS : (b + 1) * BLOCK_HEADS, g * K_PASS : (g + 1) * K_PASS]
-            sources = [w_raw[i][:, a, :].bitcast(F32) for a in range(BLOCK_HEADS)]
-            return rows, w_raw[i], sources, w_codes[i], w_scales[i], split_pairs
-
-        def load(unit):
-            nc.sync.dma_start(out=unit[1][:], in_=unit[0])
+            for tiles in (slice(0, 2), slice(2, TOKEN_TILES)):
+                shape = [P, tiles.stop - tiles.start, PAIRS]
+                gain_even = gain_sb[:, :, 0].unsqueeze(1).to_broadcast(shape)
+                gain_odd = gain_sb[:, :, 1].unsqueeze(1).to_broadcast(shape)
+                minus_gain_odd = minus_gain[:, :, 1].unsqueeze(1).to_broadcast(shape)
+                cos, sin = cos_sb[:, tiles], sin_sb[:, tiles]
+                nc.gpsimd.tensor_tensor(out=table[:, tiles, 0, :, 0], in0=cos, in1=gain_even, op=ALU.mult)
+                nc.gpsimd.tensor_tensor(out=table[:, tiles, 0, :, 1], in0=sin, in1=gain_even, op=ALU.mult)
+                nc.gpsimd.tensor_tensor(out=table[:, tiles, 1, :, 0], in0=sin, in1=minus_gain_odd, op=ALU.mult)
+                nc.gpsimd.tensor_tensor(out=table[:, tiles, 1, :, 1], in0=cos, in1=gain_odd, op=ALU.mult)
 
         def transpose_and_copy(unit):
-            sources = unit[2]
-            grouped = stage.tile([P, 4 * UNIT_COLS], BF16, name="grouped", align_bytes=64)
+            kind, n = unit
+            words = (x_raw[n] if kind == "x" else w_raw[n])[:].bitcast(F32)
+            columns = ident if kind == "x" else split_pairs
+            grouped = stage.tile([P, K], BF16, name="grouped", align_bytes=64)
             grouped_words = grouped[:].bitcast(F32).rearrange("p (b a r u) -> p b a r u", b=2, a=2, u=2)
             for b in range(2):
                 bank = tpsum.tile([P, 2, 2, P], F32, name="bank")
                 for a in range(2):
+                    first = (2 * b + a) * PASS_WORDS
                     for u in range(2):
-                        nc.tensor.transpose(bank[:, a, u, :], sources[2 * b + a][:, u::2], unit[5][:])
+                        nc.tensor.transpose(bank[:, a, u, :], words[:, first + u : first + PASS_WORDS : 2], columns[:])
                 nc.scalar.copy(out=grouped_words[:, b], in_=bank[:].rearrange("p a u r -> p a r u"))
             return grouped
 
         def quantise(unit, grouped):
-            nc.vector.quantize_mx(out=unit[3][:].bitcast(FP8X4), scales=unit[4][:], in_=grouped[:])
+            kind, n = unit
+            if kind == "x":
+                nc.vector.quantize_mx(out=x_codes[n][:].bitcast(FP8X4), scales=x_scales[n][:], in_=grouped[:])
+                return
+            block, a = divmod(n, BLOCK_HEADS)
+            cols = slice(a * HEAD_DIM, (a + 1) * HEAD_DIM)
+            for g in range(PASSES):
+                nc.vector.quantize_mx(
+                    out=w_codes[block * PASSES + g][:, cols].bitcast(FP8X4),
+                    scales=w_scales[block * PASSES + g][:, cols],
+                    in_=grouped[:, g * K_PASS : (g + 1) * K_PASS],
+                )
 
+        pieces = [(b, t, 0, BLOCK_HEADS) for b in range(BLOCKS) for t in range(TOKEN_TILES)]
+        half = BLOCK_HEADS // 2
+        pieces[:1] = [(0, 0, 0, half), (0, 0, half, half)]
+        pieces[-1:] = [(BLOCKS - 1, TOKEN_TILES - 1, 0, half), (BLOCKS - 1, TOKEN_TILES - 1, half, half)]
         accs = {}
-        squares_of = {}
         sumsq_of = {}
         inv_of = {}
+        squares_of = {}
 
         def multiply(i):
-            b, t = divmod(i, TOKEN_TILES)
+            b, t, h0, heads = pieces[i]
             acc = mpsum.tile([P, BLOCK_COLS], F32, name="acc")
+            cols = slice(h0 * HEAD_DIM, (h0 + heads) * HEAD_DIM)
             for g in range(PASSES):
                 tokens = slice(g * P, (g + 1) * P)
                 nc.tensor.matmul_mx(
-                    out=acc[:],
+                    out=acc[:, : heads * HEAD_DIM],
                     lhsT=x_codes[t][:, tokens].bitcast(FP8X4),
                     lhsT_scale=x_scales[t][:, tokens],
-                    rhs=w_codes[b * PASSES + g][:].bitcast(FP8X4),
-                    rhs_scale=w_scales[b * PASSES + g][:],
+                    rhs=w_codes[b * PASSES + g][:, cols].bitcast(FP8X4),
+                    rhs_scale=w_scales[b * PASSES + g][:, cols],
                     start=(g == 0),
                     stop=(g == PASSES - 1),
                 )
             accs[i] = acc
 
-        def sum_squares(i, heads):
+        def sum_squares(i, first, last):
             if i not in sumsq_of:
                 squares_of[i] = work.tile([P, BLOCK_COLS], F32, name="squares")
                 sumsq_of[i] = small.tile([P, BLOCK_HEADS], F32, name="sumsq")
-            for h in heads:
+            for h in range(first, last):
                 cols = slice(h * HEAD_DIM, (h + 1) * HEAD_DIM)
                 nc.scalar.activation(
                     out=squares_of[i][:, cols],
@@ -170,18 +188,25 @@ def tile_mla_pb_kernel(tc, x, wq, q_norm_w, freqs_cos, freqs_sin, out):
                 )
 
         def inverse_rms(i):
+            heads = pieces[i][3]
             inv = small.tile([P, BLOCK_HEADS], F32, name="inv")
             nc.scalar.activation(
-                out=inv[:], in_=sumsq_of[i][:], func=ACT.Abs_reciprocal_sqrt, bias=eps_sb[:], scale=1.0 / HEAD_DIM
+                out=inv[:, :heads],
+                in_=sumsq_of[i][:, :heads],
+                func=ACT.Abs_reciprocal_sqrt,
+                bias=eps_sb[:],
+                scale=1.0 / HEAD_DIM,
             )
             inv_of[i] = inv
 
-        def rotate_and_store(i):
-            b, t = divmod(i, TOKEN_TILES)
+        products_of = {}
+
+        def rotate(i):
+            b, t, h0, heads = pieces[i]
             acc = accs[i]
             inv = inv_of[i]
             products = work.tile([P, BLOCK_HEADS, 2, PAIRS, 2], F32, name="products")
-            for h in range(BLOCK_HEADS):
+            for h in range(heads):
                 nc.vector.scalar_tensor_tensor(
                     out=products[:, h].rearrange("p x j e -> p (x j) e"),
                     in0=acc[:, h * HEAD_DIM : (h + 1) * HEAD_DIM].unsqueeze(2).to_broadcast([P, HEAD_DIM, 2]),
@@ -190,43 +215,48 @@ def tile_mla_pb_kernel(tc, x, wq, q_norm_w, freqs_cos, freqs_sin, out):
                     op0=ALU.mult,
                     op1=ALU.mult,
                 )
+            products_of[i] = products
+
+        def add_and_store(i, adder):
+            b, t, h0, heads = pieces[i]
+            products = products_of[i]
             rotated = result.tile([P, BLOCK_HEADS, HEAD_DIM], F32, name="rotated")
-            adder = nc.vector if i == GROUPS - 1 else nc.gpsimd
             adder.tensor_tensor(
-                out=rotated[:],
-                in0=products[:, :, 0].rearrange("p h j e -> p h (j e)"),
-                in1=products[:, :, 1].rearrange("p h j e -> p h (j e)"),
+                out=rotated[:, :heads],
+                in0=products[:, :heads, 0].rearrange("p h j e -> p h (j e)"),
+                in1=products[:, :heads, 1].rearrange("p h j e -> p h (j e)"),
                 op=ALU.add,
             )
+            first = b * BLOCK_COLS + h0 * HEAD_DIM
             nc.sync.dma_start(
-                out=out_view[:, t, b * BLOCK_COLS : (b + 1) * BLOCK_COLS],
-                in_=rotated[:].rearrange("p h d -> p (h d)"),
+                out=out_view[:, t, first : first + heads * HEAD_DIM],
+                in_=rotated[:, :heads].rearrange("p h d -> p (h d)"),
             )
 
-        units = [w_unit(0, g) for g in range(PASSES)] + [x_unit(t) for t in range(TOKEN_TILES)]
-        units += [w_unit(b, g) for b in range(1, BLOCKS) for g in range(PASSES)]
-        for unit in units[:LOAD_LEAD]:
-            load(unit)
+        def finish(i):
+            inverse_rms(i)
+            rotate(i)
+            if i < len(pieces) - 2:
+                add_and_store(i, nc.gpsimd)
+
         done_units = 0
-        done_groups = 0
-        for run_units, run_groups in RUNS:
-            run = units[done_units : done_units + run_units]
-            for n, unit in enumerate(run):
-                if done_units + n + LOAD_LEAD < len(units):
-                    load(units[done_units + n + LOAD_LEAD])
-                quantise(unit, transpose_and_copy(unit))
-                if done_units + n == 1:
+        done_pieces = 0
+        for run_units, run_pieces in RUNS:
+            for n in range(done_units, done_units + run_units):
+                if n + LOAD_LEAD < len(units):
+                    load(units[n + LOAD_LEAD])
+                quantise(units[n], transpose_and_copy(units[n]))
+                if n == TABLE_UNIT:
                     build_table()
             done_units += run_units
-            for n in range(run_groups):
-                i = done_groups + n
+            for i in range(done_pieces, done_pieces + run_pieces):
                 multiply(i)
-                sum_squares(i, range(0, 1))
-                if n > 0:
-                    inverse_rms(i - 1)
-                    rotate_and_store(i - 1)
-                sum_squares(i, range(1, BLOCK_HEADS))
-            if run_groups:
-                inverse_rms(done_groups + run_groups - 1)
-                rotate_and_store(done_groups + run_groups - 1)
-            done_groups += run_groups
+                sum_squares(i, 0, 1)
+                if i > done_pieces:
+                    finish(i - 1)
+                sum_squares(i, 1, pieces[i][3])
+            done_pieces += run_pieces
+            if run_pieces:
+                finish(done_pieces - 1)
+        for i in range(len(pieces) - 2, len(pieces)):
+            add_and_store(i, nc.vector)

@@ -30,6 +30,9 @@ BLOCKS = HEADS // BLOCK_HEADS
 LOAD_LEAD = 8
 TABLE_UNIT = 1
 
+ADD_PERIOD = 4
+VECTOR_ADD = 3
+
 RUNS = [(5, 0), (2, 2), (2, 2), (2, 2), (2, 1), (2, 1), (2, 3), (2, 3), (2, 4), (2, 4), (1, 12)]
 
 FLOPS = 2 * TOKENS * K * HEADS * HEAD_DIM
@@ -233,10 +236,16 @@ def tile_mla_pb_kernel(tc, x, wq, q_norm_w, freqs_cos, freqs_sin, out):
                 in_=rotated[:, :heads].rearrange("p h d -> p (h d)"),
             )
 
+        vector_adds = []
+
         def finish(i):
             inverse_rms(i)
             rotate(i)
-            if i < len(pieces) - 2:
+            while vector_adds:
+                add_and_store(vector_adds.pop(), nc.vector)
+            if i % ADD_PERIOD == VECTOR_ADD or i >= len(pieces) - 2:
+                vector_adds.append(i)
+            else:
                 add_and_store(i, nc.gpsimd)
 
         done_units = 0
@@ -258,5 +267,5 @@ def tile_mla_pb_kernel(tc, x, wq, q_norm_w, freqs_cos, freqs_sin, out):
             done_pieces += run_pieces
             if run_pieces:
                 finish(done_pieces - 1)
-        for i in range(len(pieces) - 2, len(pieces)):
+        for i in vector_adds:
             add_and_store(i, nc.vector)

@@ -23,17 +23,14 @@ K_PASS = 4 * P
 PASSES = K // K_PASS
 PASS_WORDS = K_PASS // 2
 TOKEN_TILES = TOKENS // P
-BLOCK_HEADS = 4
-BLOCK_COLS = BLOCK_HEADS * HEAD_DIM
-BLOCKS = HEADS // BLOCK_HEADS
+PAIR_COLS = 2 * HEAD_DIM
+HEAD_PAIRS = HEADS // 2
+TILE_PAIRS = TOKEN_TILES // 2
 
 LOAD_LEAD = 8
-TABLE_UNIT = 1
-
-ADD_PERIOD = 4
-VECTOR_ADD = 3
-
-RUNS = [(5, 0), (2, 2), (2, 2), (2, 2), (2, 1), (2, 1), (2, 3), (2, 3), (2, 4), (2, 4), (1, 12)]
+HALVED_LOADS = 4
+VADD = 2
+FIRST_TILES = 2
 
 FLOPS = 2 * TOKENS * K * HEADS * HEAD_DIM
 
@@ -50,7 +47,7 @@ def tile_mla_pb_kernel(tc, x, wq, q_norm_w, freqs_cos, freqs_sin, out):
         const = ctx.enter_context(tc.tile_pool(name="const", bufs=1))
         raw = ctx.enter_context(tc.tile_pool(name="raw", bufs=1))
         keep = ctx.enter_context(tc.tile_pool(name="keep", bufs=1))
-        stage = ctx.enter_context(tc.tile_pool(name="stage", bufs=4))
+        stage = ctx.enter_context(tc.tile_pool(name="stage", bufs=3))
         work = ctx.enter_context(tc.tile_pool(name="work", bufs=3))
         result = ctx.enter_context(tc.tile_pool(name="result", bufs=6))
         small = ctx.enter_context(tc.tile_pool(name="small", bufs=4))
@@ -60,31 +57,41 @@ def tile_mla_pb_kernel(tc, x, wq, q_norm_w, freqs_cos, freqs_sin, out):
 
         x_codes = [keep.tile([P, K // 4], U32, name="x_codes%d" % t, align_bytes=64) for t in range(TOKEN_TILES)]
         x_scales = [keep.tile([P, K // 4], U8, name="x_scales%d" % t, align_bytes=64) for t in range(TOKEN_TILES)]
-        w_codes = [keep.tile([P, BLOCK_COLS], U32, name="w_codes%d" % i, align_bytes=64) for i in range(BLOCKS * PASSES)]
-        w_scales = [keep.tile([P, BLOCK_COLS], U8, name="w_scales%d" % i, align_bytes=64) for i in range(BLOCKS * PASSES)]
+        w_codes = [keep.tile([P, PASSES, PAIR_COLS], U32, name="w_codes%d" % i, align_bytes=64) for i in range(HEAD_PAIRS)]
+        w_scales = [keep.tile([P, PASSES, PAIR_COLS], U8, name="w_scales%d" % i, align_bytes=64) for i in range(HEAD_PAIRS)]
 
         x_raw = [raw.tile([P, K], BF16, name="x_raw%d" % t) for t in range(TOKEN_TILES)]
         w_raw = [raw.tile([P, K], BF16, name="w_raw%d" % h) for h in range(HEADS)]
-        units = [("x", 0)] + [("w", h) for h in range(BLOCK_HEADS)]
-        units += [("x", t) for t in range(1, TOKEN_TILES)] + [("w", h) for h in range(BLOCK_HEADS, HEADS)]
+        pairs = [("x", 0), ("w", 0)]
+        for n in range(1, TILE_PAIRS):
+            pairs += [("w", n), ("x", n)]
+        pairs += [("w", n) for n in range(TILE_PAIRS, HEAD_PAIRS)]
+        units = [(kind, 2 * n + m) for kind, n in pairs for m in range(2)]
 
-        def load(unit):
-            kind, n = unit
-            if kind == "x":
-                nc.sync.dma_start(out=x_raw[n][:], in_=x_view[:, n, :])
-            else:
-                nc.sync.dma_start(out=w_raw[n][:], in_=wq_view[:, n, :])
+        def load(n):
+            if n >= len(units):
+                return
+            kind, m = units[n]
+            rows = x_raw[m] if kind == "x" else w_raw[m]
+            source = x_view[:, m, :] if kind == "x" else wq_view[:, m, :]
+            width = K // 2 if n < HALVED_LOADS else K
+            for first in range(0, K, width):
+                nc.sync.dma_start(out=rows[:, first : first + width], in_=source[:, first : first + width])
 
         cos_sb = const.tile([P, TOKEN_TILES, PAIRS], BF16, name="cos_sb")
         sin_sb = const.tile([P, TOKEN_TILES, PAIRS], BF16, name="sin_sb")
         gain_rows = const.tile([P, HEAD_DIM], BF16, name="gain_rows")
         nc.vector.memset(gain_rows[:], 0.0)
         nc.scalar.dma_start(out=gain_rows[0:1, :], in_=q_norm_w.unsqueeze(0))
-        load(units[0])
-        nc.sync.dma_start(out=cos_sb[:], in_=cos_view)
-        nc.sync.dma_start(out=sin_sb[:], in_=sin_view)
-        for unit in units[1:LOAD_LEAD]:
-            load(unit)
+        load(0)
+        nc.sync.dma_start(out=cos_sb[:, :FIRST_TILES], in_=cos_view[:, :FIRST_TILES])
+        nc.sync.dma_start(out=sin_sb[:, :FIRST_TILES], in_=sin_view[:, :FIRST_TILES])
+        for n in range(1, 6):
+            load(n)
+        nc.sync.dma_start(out=cos_sb[:, FIRST_TILES:], in_=cos_view[:, FIRST_TILES:])
+        nc.sync.dma_start(out=sin_sb[:, FIRST_TILES:], in_=sin_view[:, FIRST_TILES:])
+        for n in range(6, LOAD_LEAD):
+            load(n)
 
         ident = const.tile([P, P], F32, name="ident")
         make_identity(nc, ident[:])
@@ -111,7 +118,7 @@ def tile_mla_pb_kernel(tc, x, wq, q_norm_w, freqs_cos, freqs_sin, out):
             minus_gain = const.tile([P, PAIRS, 2], F32, name="minus_gain")
             nc.scalar.copy(out=gain_sb[:], in_=gain_ps[:])
             nc.scalar.mul(out=minus_gain[:], in_=gain_ps[:], mul=-1.0)
-            for tiles in (slice(0, 2), slice(2, TOKEN_TILES)):
+            for tiles in (slice(0, FIRST_TILES), slice(FIRST_TILES, TOKEN_TILES)):
                 shape = [P, tiles.stop - tiles.start, PAIRS]
                 gain_even = gain_sb[:, :, 0].unsqueeze(1).to_broadcast(shape)
                 gain_odd = gain_sb[:, :, 1].unsqueeze(1).to_broadcast(shape)
@@ -122,150 +129,160 @@ def tile_mla_pb_kernel(tc, x, wq, q_norm_w, freqs_cos, freqs_sin, out):
                 nc.gpsimd.tensor_tensor(out=table[:, tiles, 1, :, 0], in0=sin, in1=minus_gain_odd, op=ALU.mult)
                 nc.gpsimd.tensor_tensor(out=table[:, tiles, 1, :, 1], in0=cos, in1=gain_odd, op=ALU.mult)
 
-        def transpose_and_copy(unit):
+        def transpose_and_copy(unit, grouped_words):
             kind, n = unit
             words = (x_raw[n] if kind == "x" else w_raw[n])[:].bitcast(F32)
             columns = ident if kind == "x" else split_pairs
-            grouped = stage.tile([P, K], BF16, name="grouped", align_bytes=64)
-            grouped_words = grouped[:].bitcast(F32).rearrange("p (b a r u) -> p b a r u", b=2, a=2, u=2)
             for b in range(2):
                 bank = tpsum.tile([P, 2, 2, P], F32, name="bank")
                 for a in range(2):
                     first = (2 * b + a) * PASS_WORDS
                     for u in range(2):
                         nc.tensor.transpose(bank[:, a, u, :], words[:, first + u : first + PASS_WORDS : 2], columns[:])
-                nc.scalar.copy(out=grouped_words[:, b], in_=bank[:].rearrange("p a u r -> p a r u"))
-            return grouped
+                nc.scalar.copy(out=grouped_words[:, 2 * b : 2 * b + 2], in_=bank[:].rearrange("p a u r -> p a r u"))
 
-        def quantise(unit, grouped):
-            kind, n = unit
-            if kind == "x":
-                nc.vector.quantize_mx(out=x_codes[n][:].bitcast(FP8X4), scales=x_scales[n][:], in_=grouped[:])
-                return
-            block, a = divmod(n, BLOCK_HEADS)
-            cols = slice(a * HEAD_DIM, (a + 1) * HEAD_DIM)
+        def prepare_x(n):
+            grouped = stage.tile([P, PASSES, P, 4], BF16, name="x_grouped", align_bytes=64)
+            words = grouped[:].rearrange("p g r v -> p (g r v)").bitcast(F32)
+            transpose_and_copy(("x", n), words.rearrange("p (g r u) -> p g r u", g=PASSES, u=2))
+            nc.vector.quantize_mx(
+                out=x_codes[n][:].bitcast(FP8X4), scales=x_scales[n][:], in_=grouped[:].rearrange("p g r v -> p (g r v)")
+            )
+
+        def prepare_w(i):
+            grouped = stage.tile([P, PASSES, 2, P, 4], BF16, name="w_grouped", align_bytes=64)
+            words = grouped[:].rearrange("p g h r v -> p (g h r v)").bitcast(F32)
+            words = words.rearrange("p (g h r u) -> p g h r u", g=PASSES, h=2, u=2)
+            for a in range(2):
+                transpose_and_copy(("w", 2 * i + a), words[:, :, a])
             for g in range(PASSES):
                 nc.vector.quantize_mx(
-                    out=w_codes[block * PASSES + g][:, cols].bitcast(FP8X4),
-                    scales=w_scales[block * PASSES + g][:, cols],
-                    in_=grouped[:, g * K_PASS : (g + 1) * K_PASS],
+                    out=w_codes[i][:, g].bitcast(FP8X4),
+                    scales=w_scales[i][:, g],
+                    in_=grouped[:, g].rearrange("p h r v -> p (h r v)"),
                 )
 
-        pieces = [(b, t, 0, BLOCK_HEADS) for b in range(BLOCKS) for t in range(TOKEN_TILES)]
-        half = BLOCK_HEADS // 2
-        pieces[:1] = [(0, 0, 0, half), (0, 0, half, half)]
-        pieces[-1:] = [(BLOCKS - 1, TOKEN_TILES - 1, 0, half), (BLOCKS - 1, TOKEN_TILES - 1, half, half)]
+        def slots(piece):
+            tile_pair, head_pair = piece
+            return [(2 * tile_pair + s, 2 * head_pair + a) for s in range(2) for a in range(2)]
+
         accs = {}
         sumsq_of = {}
         inv_of = {}
         squares_of = {}
+        products_of = {}
 
-        def multiply(i):
-            b, t, h0, heads = pieces[i]
-            acc = mpsum.tile([P, BLOCK_COLS], F32, name="acc")
-            cols = slice(h0 * HEAD_DIM, (h0 + heads) * HEAD_DIM)
-            for g in range(PASSES):
-                tokens = slice(g * P, (g + 1) * P)
-                nc.tensor.matmul_mx(
-                    out=acc[:, : heads * HEAD_DIM],
-                    lhsT=x_codes[t][:, tokens].bitcast(FP8X4),
-                    lhsT_scale=x_scales[t][:, tokens],
-                    rhs=w_codes[b * PASSES + g][:, cols].bitcast(FP8X4),
-                    rhs_scale=w_scales[b * PASSES + g][:, cols],
-                    start=(g == 0),
-                    stop=(g == PASSES - 1),
-                )
-            accs[i] = acc
+        def multiply(piece):
+            tile_pair, head_pair = piece
+            acc = mpsum.tile([P, 4 * HEAD_DIM], F32, name="acc")
+            for s in range(2):
+                for g in range(PASSES):
+                    tokens = slice(g * P, (g + 1) * P)
+                    nc.tensor.matmul_mx(
+                        out=acc[:, s * PAIR_COLS : (s + 1) * PAIR_COLS],
+                        lhsT=x_codes[2 * tile_pair + s][:, tokens].bitcast(FP8X4),
+                        lhsT_scale=x_scales[2 * tile_pair + s][:, tokens],
+                        rhs=w_codes[head_pair][:, g].bitcast(FP8X4),
+                        rhs_scale=w_scales[head_pair][:, g],
+                        start=(g == 0),
+                        stop=(g == PASSES - 1),
+                    )
+            accs[piece] = acc
 
-        def sum_squares(i, first, last):
-            if i not in sumsq_of:
-                squares_of[i] = work.tile([P, BLOCK_COLS], F32, name="squares")
-                sumsq_of[i] = small.tile([P, BLOCK_HEADS], F32, name="sumsq")
-            for h in range(first, last):
-                cols = slice(h * HEAD_DIM, (h + 1) * HEAD_DIM)
+        def sum_squares(piece, first, last):
+            if piece not in sumsq_of:
+                squares_of[piece] = work.tile([P, 4 * HEAD_DIM], F32, name="squares")
+                sumsq_of[piece] = small.tile([P, 4], F32, name="sumsq")
+            for n in range(first, last):
+                cols = slice(n * HEAD_DIM, (n + 1) * HEAD_DIM)
                 nc.scalar.activation(
-                    out=squares_of[i][:, cols],
-                    in_=accs[i][:, cols],
+                    out=squares_of[piece][:, cols],
+                    in_=accs[piece][:, cols],
                     func=ACT.Square,
-                    accum_out=sumsq_of[i][:, h : h + 1],
+                    accum_out=sumsq_of[piece][:, n : n + 1],
                 )
 
-        def inverse_rms(i):
-            heads = pieces[i][3]
-            inv = small.tile([P, BLOCK_HEADS], F32, name="inv")
+        def inverse_rms(piece):
+            inv = small.tile([P, 4], F32, name="inv")
             nc.scalar.activation(
-                out=inv[:, :heads],
-                in_=sumsq_of[i][:, :heads],
+                out=inv[:],
+                in_=sumsq_of[piece][:],
                 func=ACT.Abs_reciprocal_sqrt,
                 bias=eps_sb[:],
                 scale=1.0 / HEAD_DIM,
             )
-            inv_of[i] = inv
+            inv_of[piece] = inv
 
-        products_of = {}
-
-        def rotate(i):
-            b, t, h0, heads = pieces[i]
-            acc = accs[i]
-            inv = inv_of[i]
-            products = work.tile([P, BLOCK_HEADS, 2, PAIRS, 2], F32, name="products")
-            for h in range(heads):
+        def rotate(piece, first, last):
+            if first == 0:
+                products_of[piece] = work.tile([P, 4, 2, PAIRS, 2], F32, name="products")
+            for n in range(first, last):
+                t = slots(piece)[n][0]
                 nc.vector.scalar_tensor_tensor(
-                    out=products[:, h].rearrange("p x j e -> p (x j) e"),
-                    in0=acc[:, h * HEAD_DIM : (h + 1) * HEAD_DIM].unsqueeze(2).to_broadcast([P, HEAD_DIM, 2]),
-                    scalar=inv[:, h : h + 1],
+                    out=products_of[piece][:, n].rearrange("p x j e -> p (x j) e"),
+                    in0=accs[piece][:, n * HEAD_DIM : (n + 1) * HEAD_DIM].unsqueeze(2).to_broadcast([P, HEAD_DIM, 2]),
+                    scalar=inv_of[piece][:, n : n + 1],
                     in1=table[:, t].rearrange("p x j e -> p (x j) e"),
                     op0=ALU.mult,
                     op1=ALU.mult,
                 )
-            products_of[i] = products
 
-        def add_and_store(i, adder):
-            b, t, h0, heads = pieces[i]
-            products = products_of[i]
-            rotated = result.tile([P, BLOCK_HEADS, HEAD_DIM], F32, name="rotated")
+        def add_and_store(piece, adder):
+            tile_pair, head_pair = piece
+            products = products_of[piece]
+            rotated = result.tile([P, 4, HEAD_DIM], F32, name="rotated")
             adder.tensor_tensor(
-                out=rotated[:, :heads],
-                in0=products[:, :heads, 0].rearrange("p h j e -> p h (j e)"),
-                in1=products[:, :heads, 1].rearrange("p h j e -> p h (j e)"),
+                out=rotated[:],
+                in0=products[:, :, 0].rearrange("p n j e -> p n (j e)"),
+                in1=products[:, :, 1].rearrange("p n j e -> p n (j e)"),
                 op=ALU.add,
             )
-            first = b * BLOCK_COLS + h0 * HEAD_DIM
             nc.sync.dma_start(
-                out=out_view[:, t, first : first + heads * HEAD_DIM],
-                in_=rotated[:, :heads].rearrange("p h d -> p (h d)"),
+                out=out_view[:, 2 * tile_pair : 2 * tile_pair + 2, head_pair * PAIR_COLS : (head_pair + 1) * PAIR_COLS],
+                in_=rotated[:].rearrange("p (s a) d -> p s (a d)", s=2),
             )
 
-        vector_adds = []
+        seen = {"x": [], "w": []}
+        batches = []
+        for kind, n in pairs:
+            seen[kind].append(n)
+            others = seen["w" if kind == "x" else "x"]
+            batches.append([(n, m) if kind == "x" else (m, n) for m in others])
 
-        def finish(i):
-            inverse_rms(i)
-            rotate(i)
-            while vector_adds:
-                add_and_store(vector_adds.pop(), nc.vector)
-            if i % ADD_PERIOD == VECTOR_ADD or i >= len(pieces) - 2:
-                vector_adds.append(i)
-            else:
-                add_and_store(i, nc.gpsimd)
-
-        done_units = 0
-        done_pieces = 0
-        for run_units, run_pieces in RUNS:
-            for n in range(done_units, done_units + run_units):
-                if n + LOAD_LEAD < len(units):
-                    load(units[n + LOAD_LEAD])
-                quantise(units[n], transpose_and_copy(units[n]))
-                if n == TABLE_UNIT:
+        late = []
+        for k in range(len(pairs) + 1):
+            if k < len(pairs):
+                kind, n = pairs[k]
+                load(2 * k + LOAD_LEAD)
+                load(2 * k + 1 + LOAD_LEAD)
+                if kind == "x":
+                    prepare_x(2 * n)
+                    prepare_x(2 * n + 1)
+                else:
+                    prepare_w(n)
+                if k == 0:
                     build_table()
-            done_units += run_units
-            for i in range(done_pieces, done_pieces + run_pieces):
-                multiply(i)
-                sum_squares(i, 0, 1)
-                if i > done_pieces:
-                    finish(i - 1)
-                sum_squares(i, 1, pieces[i][3])
-            done_pieces += run_pieces
-            if run_pieces:
-                finish(done_pieces - 1)
-        for i in vector_adds:
-            add_and_store(i, nc.vector)
+            for piece in late:
+                rotate(piece, 3, 4)
+                add_and_store(piece, nc.gpsimd)
+            late = []
+            batch = batches[k - 1] if k else []
+            for i, piece in enumerate(batch):
+                multiply(piece)
+                sum_squares(piece, 0, 1)
+                if i:
+                    inverse_rms(batch[i - 1])
+                    rotate(batch[i - 1], 0, 4)
+                    if len(batch) < 4 or i - 1 != VADD % 4:
+                        add_and_store(batch[i - 1], nc.gpsimd)
+                sum_squares(piece, 1, 4)
+            if batch:
+                inverse_rms(batch[-1])
+                last = k == len(pairs)
+                rotate(batch[-1], 0, 4 if last else 3)
+                if len(batch) == 4:
+                    add_and_store(batch[VADD], nc.vector)
+                if last:
+                    add_and_store(batch[-1], nc.vector)
+                else:
+                    late = [batch[-1]]

@@ -29,7 +29,7 @@ TILE_PAIRS = TOKEN_TILES // 2
 
 LOAD_LEAD = 8
 HALVED_LOADS = 4
-VADD = 2
+VECTOR_ADDED = 2
 FIRST_TILES = 2
 
 FLOPS = 2 * TOKENS * K * HEADS * HEAD_DIM
@@ -149,18 +149,23 @@ def tile_mla_pb_kernel(tc, x, wq, q_norm_w, freqs_cos, freqs_sin, out):
                 out=x_codes[n][:].bitcast(FP8X4), scales=x_scales[n][:], in_=grouped[:].rearrange("p g r v -> p (g r v)")
             )
 
-        def prepare_w(i):
-            grouped = stage.tile([P, PASSES, 2, P, 4], BF16, name="w_grouped", align_bytes=64)
+        w_grouped = {}
+
+        def prepare_w(n):
+            i, a = divmod(n, 2)
+            if a == 0:
+                w_grouped[i] = stage.tile([P, PASSES, 2, P, 4], BF16, name="w_grouped", align_bytes=64)
+            grouped = w_grouped[i]
             words = grouped[:].rearrange("p g h r v -> p (g h r v)").bitcast(F32)
             words = words.rearrange("p (g h r u) -> p g h r u", g=PASSES, h=2, u=2)
-            for a in range(2):
-                transpose_and_copy(("w", 2 * i + a), words[:, :, a])
-            for g in range(PASSES):
-                nc.vector.quantize_mx(
-                    out=w_codes[i][:, g].bitcast(FP8X4),
-                    scales=w_scales[i][:, g],
-                    in_=grouped[:, g].rearrange("p h r v -> p (h r v)"),
-                )
+            transpose_and_copy(("w", n), words[:, :, a])
+            if a == 1:
+                for g in range(PASSES):
+                    nc.vector.quantize_mx(
+                        out=w_codes[i][:, g].bitcast(FP8X4),
+                        scales=w_scales[i][:, g],
+                        in_=grouped[:, g].rearrange("p h r v -> p (h r v)"),
+                    )
 
         def slots(piece):
             tile_pair, head_pair = piece
@@ -249,40 +254,51 @@ def tile_mla_pb_kernel(tc, x, wq, q_norm_w, freqs_cos, freqs_sin, out):
             others = seen["w" if kind == "x" else "x"]
             batches.append([(n, m) if kind == "x" else (m, n) for m in others])
 
+        steps = [[] for n in range(len(units) + 3)]
+        for k, batch in enumerate(batches):
+            half = (len(batch) + 1) // 2
+            steps[2 * k + 3] += batch[:half]
+            steps[2 * k + 4] += batch[half:]
+        vector_added = [batch[VECTOR_ADDED] for batch in batches if len(batch) == 4]
+        final = batches[-1][-1]
         late = []
-        for k in range(len(pairs) + 1):
-            if k < len(pairs):
-                kind, n = pairs[k]
-                load(2 * k + LOAD_LEAD)
-                load(2 * k + 1 + LOAD_LEAD)
+        waiting = []
+
+        def close(piece, slots_now):
+            inverse_rms(piece)
+            rotate(piece, 0, slots_now)
+            while waiting:
+                add_and_store(waiting.pop(), nc.vector)
+            if slots_now < 4:
+                late.append(piece)
+            elif piece in vector_added or piece == final:
+                waiting.append(piece)
+            else:
+                add_and_store(piece, nc.gpsimd)
+
+        for n in range(len(steps)):
+            if n < len(units):
+                load(n + LOAD_LEAD)
+                kind, m = units[n]
                 if kind == "x":
-                    prepare_x(2 * n)
-                    prepare_x(2 * n + 1)
+                    prepare_x(m)
                 else:
-                    prepare_w(n)
-                if k == 0:
+                    prepare_w(m)
+                if n == 1:
                     build_table()
-            for piece in late:
+            while late:
+                piece = late.pop()
                 rotate(piece, 3, 4)
                 add_and_store(piece, nc.gpsimd)
-            late = []
-            batch = batches[k - 1] if k else []
-            for i, piece in enumerate(batch):
+            for i, piece in enumerate(steps[n]):
                 multiply(piece)
                 sum_squares(piece, 0, 1)
                 if i:
-                    inverse_rms(batch[i - 1])
-                    rotate(batch[i - 1], 0, 4)
-                    if len(batch) < 4 or i - 1 != VADD % 4:
-                        add_and_store(batch[i - 1], nc.gpsimd)
+                    close(steps[n][i - 1], 4)
                 sum_squares(piece, 1, 4)
-            if batch:
-                inverse_rms(batch[-1])
-                last = k == len(pairs)
-                rotate(batch[-1], 0, 4 if last else 3)
-                if len(batch) == 4:
-                    add_and_store(batch[VADD], nc.vector)
-                if last:
-                    add_and_store(batch[-1], nc.vector)
-                else:
-                    late = [batch[-1]]
+            if steps[n]:
+                quantised_next = n + 1 < len(units) and (units[n + 1][0] == "x" or units[n + 1][1] % 2 == 1)
+                hold = quantised_next and steps[n][-1] not in vector_added
+                close(steps[n][-1], 3 if hold else 4)
+        for piece in waiting:
+            add_and_store(piece, nc.vector)

@@ -218,11 +218,9 @@ def tile_mla_pb_kernel(tc, x, wq, q_norm_w, freqs_cos, freqs_sin, out):
             )
             inv_of[piece] = inv
 
-        def rotate(piece, first, last):
-            if first == 0:
-                products_of[piece] = work.tile([P, 4, 2, PAIRS, 2], F32, name="products")
-            for n in range(first, last):
-                t = slots(piece)[n][0]
+        def rotate(piece):
+            products_of[piece] = work.tile([P, 4, 2, PAIRS, 2], F32, name="products")
+            for n, (t, h) in enumerate(slots(piece)):
                 nc.vector.scalar_tensor_tensor(
                     out=products_of[piece][:, n].rearrange("p x j e -> p (x j) e"),
                     in0=accs[piece][:, n * HEAD_DIM : (n + 1) * HEAD_DIM].unsqueeze(2).to_broadcast([P, HEAD_DIM, 2]),
@@ -261,17 +259,14 @@ def tile_mla_pb_kernel(tc, x, wq, q_norm_w, freqs_cos, freqs_sin, out):
             steps[2 * k + 4] += batch[half:]
         vector_added = [batch[VECTOR_ADDED] for batch in batches if len(batch) == 4]
         final = batches[-1][-1]
-        late = []
         waiting = []
 
-        def close(piece, slots_now):
+        def close(piece):
             inverse_rms(piece)
-            rotate(piece, 0, slots_now)
+            rotate(piece)
             while waiting:
                 add_and_store(waiting.pop(), nc.vector)
-            if slots_now < 4:
-                late.append(piece)
-            elif piece in vector_added or piece == final:
+            if piece in vector_added or piece == final:
                 waiting.append(piece)
             else:
                 add_and_store(piece, nc.gpsimd)
@@ -286,19 +281,13 @@ def tile_mla_pb_kernel(tc, x, wq, q_norm_w, freqs_cos, freqs_sin, out):
                     prepare_w(m)
                 if n == 1:
                     build_table()
-            while late:
-                piece = late.pop()
-                rotate(piece, 3, 4)
-                add_and_store(piece, nc.gpsimd)
             for i, piece in enumerate(steps[n]):
                 multiply(piece)
                 sum_squares(piece, 0, 1)
                 if i:
-                    close(steps[n][i - 1], 4)
+                    close(steps[n][i - 1])
                 sum_squares(piece, 1, 4)
             if steps[n]:
-                quantised_next = n + 1 < len(units) and (units[n + 1][0] == "x" or units[n + 1][1] % 2 == 1)
-                hold = quantised_next and steps[n][-1] not in vector_added
-                close(steps[n][-1], 3 if hold else 4)
+                close(steps[n][-1])
         for piece in waiting:
             add_and_store(piece, nc.vector)

@@ -177,22 +177,21 @@ def tile_mla_pb_kernel(tc, x, wq, q_norm_w, freqs_cos, freqs_sin, out):
         squares_of = {}
         products_of = {}
 
-        def multiply(piece):
+        def multiply(piece, s):
             tile_pair, head_pair = piece
-            acc = mpsum.tile([P, 4 * HEAD_DIM], F32, name="acc")
-            for s in range(2):
-                for g in range(PASSES):
-                    tokens = slice(g * P, (g + 1) * P)
-                    nc.tensor.matmul_mx(
-                        out=acc[:, s * PAIR_COLS : (s + 1) * PAIR_COLS],
-                        lhsT=x_codes[2 * tile_pair + s][:, tokens].bitcast(FP8X4),
-                        lhsT_scale=x_scales[2 * tile_pair + s][:, tokens],
-                        rhs=w_codes[head_pair][:, g].bitcast(FP8X4),
-                        rhs_scale=w_scales[head_pair][:, g],
-                        start=(g == 0),
-                        stop=(g == PASSES - 1),
-                    )
-            accs[piece] = acc
+            if s == 0:
+                accs[piece] = mpsum.tile([P, 4 * HEAD_DIM], F32, name="acc")
+            for g in range(PASSES):
+                tokens = slice(g * P, (g + 1) * P)
+                nc.tensor.matmul_mx(
+                    out=accs[piece][:, s * PAIR_COLS : (s + 1) * PAIR_COLS],
+                    lhsT=x_codes[2 * tile_pair + s][:, tokens].bitcast(FP8X4),
+                    lhsT_scale=x_scales[2 * tile_pair + s][:, tokens],
+                    rhs=w_codes[head_pair][:, g].bitcast(FP8X4),
+                    rhs_scale=w_scales[head_pair][:, g],
+                    start=(g == 0),
+                    stop=(g == PASSES - 1),
+                )
 
         def sum_squares(piece, first, last):
             if piece not in sumsq_of:
@@ -254,22 +253,25 @@ def tile_mla_pb_kernel(tc, x, wq, q_norm_w, freqs_cos, freqs_sin, out):
 
         steps = [[] for n in range(len(units) + 3)]
         for k, batch in enumerate(batches):
-            half = (len(batch) + 1) // 2
-            steps[2 * k + 3] += batch[:half]
-            steps[2 * k + 4] += batch[half:]
+            halves = [(piece, s) for piece in batch for s in range(2)]
+            steps[2 * k + 3] += halves[: len(batch)]
+            steps[2 * k + 4] += halves[len(batch) :]
         vector_added = [batch[VECTOR_ADDED] for batch in batches if len(batch) == 4]
         final = batches[-1][-1]
+        full = []
         waiting = []
 
-        def close(piece):
-            inverse_rms(piece)
-            rotate(piece)
-            while waiting:
-                add_and_store(waiting.pop(), nc.vector)
-            if piece in vector_added or piece == final:
-                waiting.append(piece)
-            else:
-                add_and_store(piece, nc.gpsimd)
+        def close():
+            while full:
+                piece = full.pop()
+                inverse_rms(piece)
+                rotate(piece)
+                while waiting:
+                    add_and_store(waiting.pop(), nc.vector)
+                if piece in vector_added or piece == final:
+                    waiting.append(piece)
+                else:
+                    add_and_store(piece, nc.gpsimd)
 
         for n in range(len(steps)):
             if n < len(units):
@@ -281,13 +283,13 @@ def tile_mla_pb_kernel(tc, x, wq, q_norm_w, freqs_cos, freqs_sin, out):
                     prepare_w(m)
                 if n == 1:
                     build_table()
-            for i, piece in enumerate(steps[n]):
-                multiply(piece)
-                sum_squares(piece, 0, 1)
-                if i:
-                    close(steps[n][i - 1])
-                sum_squares(piece, 1, 4)
-            if steps[n]:
-                close(steps[n][-1])
+            for piece, s in steps[n]:
+                multiply(piece, s)
+                sum_squares(piece, 2 * s, 2 * s + 1)
+                close()
+                sum_squares(piece, 2 * s + 1, 2 * s + 2)
+                if s == 1:
+                    full.append(piece)
+            close()
         for piece in waiting:
             add_and_store(piece, nc.vector)

@@ -28,7 +28,7 @@ HEAD_PAIRS = HEADS // 2
 TILE_PAIRS = TOKEN_TILES // 2
 
 LOAD_LEAD = 8
-HALVED_LOADS = 4
+HALVED_LOADS = 6
 VECTOR_ADDED = 2
 FIRST_TILES = 2
 
@@ -254,8 +254,9 @@ def tile_mla_pb_kernel(tc, x, wq, q_norm_w, freqs_cos, freqs_sin, out):
         steps = [[] for n in range(len(units) + 3)]
         for k, batch in enumerate(batches):
             halves = [(piece, s) for piece in batch for s in range(2)]
-            steps[2 * k + 3] += halves[: len(batch)]
-            steps[2 * k + 4] += halves[len(batch) :]
+            early = len(batch) + len(batch) // 2
+            steps[2 * k + 3] += halves[:early]
+            steps[2 * k + 4] += halves[early:]
         vector_added = [batch[VECTOR_ADDED] for batch in batches if len(batch) == 4]
         final = batches[-1][-1]
         full = []
@@ -285,10 +286,10 @@ def tile_mla_pb_kernel(tc, x, wq, q_norm_w, freqs_cos, freqs_sin, out):
                     build_table()
             for piece, s in steps[n]:
                 multiply(piece, s)
-                sum_squares(piece, 2 * s, 2 * s + 1)
-                close()
-                sum_squares(piece, 2 * s + 1, 2 * s + 2)
                 if s == 1:
+                    sum_squares(piece, 0, 1)
+                    close()
+                    sum_squares(piece, 1, 4)
                     full.append(piece)
             close()
         for piece in waiting:

from contextlib import ExitStack

import concourse.mybir as mybir
from concourse.masks import make_identity

FP8X4 = mybir.dt.float8_e4m3fn_x4
BF16 = mybir.dt.bfloat16
F32 = mybir.dt.float32
U32 = mybir.dt.uint32
U8 = mybir.dt.uint8
ACT = mybir.ActivationFunctionType
ALU = mybir.AluOpType

P = 128
TOKENS = 1024
K = 2048
HEADS = 16
HEAD_DIM = 128
PAIRS = HEAD_DIM // 2
EPS = 1e-6

K_PASS = 4 * P
PASSES = K // K_PASS
PASS_WORDS = K_PASS // 2
TOKEN_TILES = TOKENS // P
PAIR_COLS = 2 * HEAD_DIM
HEAD_PAIRS = HEADS // 2
TILE_PAIRS = TOKEN_TILES // 2

LOAD_LEAD = 8
HALVED_LOADS = 6
VECTOR_ADDED = 2
FIRST_TILES = 2

FLOPS = 2 * TOKENS * K * HEADS * HEAD_DIM


def tile_mla_pb_kernel(tc, x, wq, q_norm_w, freqs_cos, freqs_sin, out):
    nc = tc.nc
    x_view = x.rearrange("b (p t) k -> p (b t) k", t=TOKEN_TILES)
    cos_view = freqs_cos.rearrange("(p t) j -> p t j", t=TOKEN_TILES)
    sin_view = freqs_sin.rearrange("(p t) j -> p t j", t=TOKEN_TILES)
    out_view = out.rearrange("b (p t) h d -> p (b t) (h d)", t=TOKEN_TILES)
    wq_view = wq.rearrange("(h p) k -> p h k", p=P)

    with ExitStack() as ctx:
        const = ctx.enter_context(tc.tile_pool(name="const", bufs=1))
        raw = ctx.enter_context(tc.tile_pool(name="raw", bufs=1))
        keep = ctx.enter_context(tc.tile_pool(name="keep", bufs=1))
        stage = ctx.enter_context(tc.tile_pool(name="stage", bufs=3))
        work = ctx.enter_context(tc.tile_pool(name="work", bufs=3))
        result = ctx.enter_context(tc.tile_pool(name="result", bufs=6))
        small = ctx.enter_context(tc.tile_pool(name="small", bufs=4))
        tpsum = ctx.enter_context(tc.psum_pool(name="tpsum", bufs=4))
        mpsum = ctx.enter_context(tc.psum_pool(name="mpsum", bufs=4))
        ctx.enter_context(tc.manual_schedule())

        x_codes = [keep.tile([P, K // 4], U32, name="x_codes%d" % t, align_bytes=64) for t in range(TOKEN_TILES)]
        x_scales = [keep.tile([P, K // 4], U8, name="x_scales%d" % t, align_bytes=64) for t in range(TOKEN_TILES)]
        w_codes = [keep.tile([P, PASSES, PAIR_COLS], U32, name="w_codes%d" % i, align_bytes=64) for i in range(HEAD_PAIRS)]
        w_scales = [keep.tile([P, PASSES, PAIR_COLS], U8, name="w_scales%d" % i, align_bytes=64) for i in range(HEAD_PAIRS)]

        x_raw = [raw.tile([P, K], BF16, name="x_raw%d" % t) for t in range(TOKEN_TILES)]
        w_raw = [raw.tile([P, K], BF16, name="w_raw%d" % h) for h in range(HEADS)]
        pairs = [("x", 0), ("w", 0)]
        for n in range(1, TILE_PAIRS):
            pairs += [("w", n), ("x", n)]
        pairs += [("w", n) for n in range(TILE_PAIRS, HEAD_PAIRS)]
        units = [(kind, 2 * n + m) for kind, n in pairs for m in range(2)]

        def load(n):
            if n >= len(units):
                return
            kind, m = units[n]
            rows = x_raw[m] if kind == "x" else w_raw[m]
            source = x_view[:, m, :] if kind == "x" else wq_view[:, m, :]
            width = K // 2 if n < HALVED_LOADS else K
            for first in range(0, K, width):
                nc.sync.dma_start(out=rows[:, first : first + width], in_=source[:, first : first + width])

        cos_sb = const.tile([P, TOKEN_TILES, PAIRS], BF16, name="cos_sb")
        sin_sb = const.tile([P, TOKEN_TILES, PAIRS], BF16, name="sin_sb")
        gain_rows = const.tile([P, HEAD_DIM], BF16, name="gain_rows")
        nc.vector.memset(gain_rows[:], 0.0)
        nc.scalar.dma_start(out=gain_rows[0:1, :], in_=q_norm_w.unsqueeze(0))
        load(0)
        nc.sync.dma_start(out=cos_sb[:, :FIRST_TILES], in_=cos_view[:, :FIRST_TILES])
        nc.sync.dma_start(out=sin_sb[:, :FIRST_TILES], in_=sin_view[:, :FIRST_TILES])
        for n in range(1, 6):
            load(n)
        nc.sync.dma_start(out=cos_sb[:, FIRST_TILES:], in_=cos_view[:, FIRST_TILES:])
        nc.sync.dma_start(out=sin_sb[:, FIRST_TILES:], in_=sin_view[:, FIRST_TILES:])
        for n in range(6, LOAD_LEAD):
            load(n)

        ident = const.tile([P, P], F32, name="ident")
        make_identity(nc, ident[:])
        split_pairs = const.tile([P, P], F32, name="split_pairs")
        nc.vector.tensor_copy(
            out=split_pairs[:].rearrange("p (e j) -> p e j", e=2), in_=ident[:].rearrange("p (j e) -> p e j", e=2)
        )
        eps_sb = const.tile([P, 1], F32, name="eps_sb")
        nc.vector.memset(eps_sb[:], EPS)
        warm = const.tile([P, 1], F32, name="warm")
        nc.scalar.activation(out=warm[:], in_=eps_sb[:], func=ACT.Abs_reciprocal_sqrt)

        ones = const.tile([P, P], BF16, name="ones")
        nc.vector.memset(ones[:], 1.0)

        table = const.tile([P, TOKEN_TILES, 2, PAIRS, 2], F32, name="table")

        def build_table():
            gain_ps = tpsum.tile([P, PAIRS, 2], F32, name="gain_ps", tag="bank")
            nc.tensor.matmul(
                out=gain_ps[:].rearrange("p j e -> p (j e)"), lhsT=ones[:], rhs=gain_rows[:], start=True, stop=True
            )
            gain_sb = const.tile([P, PAIRS, 2], F32, name="gain_sb")
            minus_gain = const.tile([P, PAIRS, 2], F32, name="minus_gain")
            nc.scalar.copy(out=gain_sb[:], in_=gain_ps[:])
            nc.scalar.mul(out=minus_gain[:], in_=gain_ps[:], mul=-1.0)
            for tiles in (slice(0, FIRST_TILES), slice(FIRST_TILES, TOKEN_TILES)):
                shape = [P, tiles.stop - tiles.start, PAIRS]
                gain_even = gain_sb[:, :, 0].unsqueeze(1).to_broadcast(shape)
                gain_odd = gain_sb[:, :, 1].unsqueeze(1).to_broadcast(shape)
                minus_gain_odd = minus_gain[:, :, 1].unsqueeze(1).to_broadcast(shape)
                cos, sin = cos_sb[:, tiles], sin_sb[:, tiles]
                nc.gpsimd.tensor_tensor(out=table[:, tiles, 0, :, 0], in0=cos, in1=gain_even, op=ALU.mult)
                nc.gpsimd.tensor_tensor(out=table[:, tiles, 0, :, 1], in0=sin, in1=gain_even, op=ALU.mult)
                nc.gpsimd.tensor_tensor(out=table[:, tiles, 1, :, 0], in0=sin, in1=minus_gain_odd, op=ALU.mult)
                nc.gpsimd.tensor_tensor(out=table[:, tiles, 1, :, 1], in0=cos, in1=gain_odd, op=ALU.mult)

        def transpose_and_copy(unit, grouped_words):
            kind, n = unit
            words = (x_raw[n] if kind == "x" else w_raw[n])[:].bitcast(F32)
            columns = ident if kind == "x" else split_pairs
            for b in range(2):
                bank = tpsum.tile([P, 2, 2, P], F32, name="bank")
                for a in range(2):
                    first = (2 * b + a) * PASS_WORDS
                    for u in range(2):
                        nc.tensor.transpose(bank[:, a, u, :], words[:, first + u : first + PASS_WORDS : 2], columns[:])
                nc.scalar.copy(out=grouped_words[:, 2 * b : 2 * b + 2], in_=bank[:].rearrange("p a u r -> p a r u"))

        def prepare_x(n):
            grouped = stage.tile([P, PASSES, P, 4], BF16, name="x_grouped", align_bytes=64)
            words = grouped[:].rearrange("p g r v -> p (g r v)").bitcast(F32)
            transpose_and_copy(("x", n), words.rearrange("p (g r u) -> p g r u", g=PASSES, u=2))
            nc.vector.quantize_mx(
                out=x_codes[n][:].bitcast(FP8X4), scales=x_scales[n][:], in_=grouped[:].rearrange("p g r v -> p (g r v)")
            )

        w_grouped = {}

        def prepare_w(n):
            i, a = divmod(n, 2)
            if a == 0:
                w_grouped[i] = stage.tile([P, PASSES, 2, P, 4], BF16, name="w_grouped", align_bytes=64)
            grouped = w_grouped[i]
            words = grouped[:].rearrange("p g h r v -> p (g h r v)").bitcast(F32)
            words = words.rearrange("p (g h r u) -> p g h r u", g=PASSES, h=2, u=2)
            transpose_and_copy(("w", n), words[:, :, a])
            if a == 1:
                for g in range(PASSES):
                    nc.vector.quantize_mx(
                        out=w_codes[i][:, g].bitcast(FP8X4),
                        scales=w_scales[i][:, g],
                        in_=grouped[:, g].rearrange("p h r v -> p (h r v)"),
                    )

        def slots(piece):
            tile_pair, head_pair = piece
            return [(2 * tile_pair + s, 2 * head_pair + a) for s in range(2) for a in range(2)]

        accs = {}
        sumsq_of = {}
        inv_of = {}
        squares_of = {}
        products_of = {}

        def multiply(piece, s):
            tile_pair, head_pair = piece
            if s == 0:
                accs[piece] = mpsum.tile([P, 4 * HEAD_DIM], F32, name="acc")
            for g in range(PASSES):
                tokens = slice(g * P, (g + 1) * P)
                nc.tensor.matmul_mx(
                    out=accs[piece][:, s * PAIR_COLS : (s + 1) * PAIR_COLS],
                    lhsT=x_codes[2 * tile_pair + s][:, tokens].bitcast(FP8X4),
                    lhsT_scale=x_scales[2 * tile_pair + s][:, tokens],
                    rhs=w_codes[head_pair][:, g].bitcast(FP8X4),
                    rhs_scale=w_scales[head_pair][:, g],
                    start=(g == 0),
                    stop=(g == PASSES - 1),
                )

        def sum_squares(piece, first, last):
            if piece not in sumsq_of:
                squares_of[piece] = work.tile([P, 4 * HEAD_DIM], F32, name="squares")
                sumsq_of[piece] = small.tile([P, 4], F32, name="sumsq")
            for n in range(first, last):
                cols = slice(n * HEAD_DIM, (n + 1) * HEAD_DIM)
                nc.scalar.activation(
                    out=squares_of[piece][:, cols],
                    in_=accs[piece][:, cols],
                    func=ACT.Square,
                    accum_out=sumsq_of[piece][:, n : n + 1],
                )

        def inverse_rms(piece):
            inv = small.tile([P, 4], F32, name="inv")
            nc.scalar.activation(
                out=inv[:],
                in_=sumsq_of[piece][:],
                func=ACT.Abs_reciprocal_sqrt,
                bias=eps_sb[:],
                scale=1.0 / HEAD_DIM,
            )
            inv_of[piece] = inv

        def rotate(piece):
            products_of[piece] = work.tile([P, 4, 2, PAIRS, 2], F32, name="products")
            for n, (t, h) in enumerate(slots(piece)):
                nc.vector.scalar_tensor_tensor(
                    out=products_of[piece][:, n].rearrange("p x j e -> p (x j) e"),
                    in0=accs[piece][:, n * HEAD_DIM : (n + 1) * HEAD_DIM].unsqueeze(2).to_broadcast([P, HEAD_DIM, 2]),
                    scalar=inv_of[piece][:, n : n + 1],
                    in1=table[:, t].rearrange("p x j e -> p (x j) e"),
                    op0=ALU.mult,
                    op1=ALU.mult,
                )

        def add_and_store(piece, adder):
            tile_pair, head_pair = piece
            products = products_of[piece]
            rotated = result.tile([P, 4, HEAD_DIM], F32, name="rotated")
            adder.tensor_tensor(
                out=rotated[:],
                in0=products[:, :, 0].rearrange("p n j e -> p n (j e)"),
                in1=products[:, :, 1].rearrange("p n j e -> p n (j e)"),
                op=ALU.add,
            )
            nc.sync.dma_start(
                out=out_view[:, 2 * tile_pair : 2 * tile_pair + 2, head_pair * PAIR_COLS : (head_pair + 1) * PAIR_COLS],
                in_=rotated[:].rearrange("p (s a) d -> p s (a d)", s=2),
            )

        seen = {"x": [], "w": []}
        batches = []
        for kind, n in pairs:
            seen[kind].append(n)
            others = seen["w" if kind == "x" else "x"]
            batches.append([(n, m) if kind == "x" else (m, n) for m in others])

        steps = [[] for n in range(len(units) + 3)]
        for k, batch in enumerate(batches):
            halves = [(piece, s) for piece in batch for s in range(2)]
            early = len(batch) + len(batch) // 2
            steps[2 * k + 3] += halves[:early]
            steps[2 * k + 4] += halves[early:]
        vector_added = [batch[VECTOR_ADDED] for batch in batches if len(batch) == 4]
        final = batches[-1][-1]
        full = []
        waiting = []

        def close():
            while full:
                piece = full.pop()
                inverse_rms(piece)
                rotate(piece)
                while waiting:
                    add_and_store(waiting.pop(), nc.vector)
                if piece in vector_added or piece == final:
                    waiting.append(piece)
                else:
                    add_and_store(piece, nc.gpsimd)

        for n in range(len(steps)):
            if n < len(units):
                load(n + LOAD_LEAD)
                kind, m = units[n]
                if kind == "x":
                    prepare_x(m)
                else:
                    prepare_w(m)
                if n == 1:
                    build_table()
            for piece, s in steps[n]:
                multiply(piece, s)
                if s == 1:
                    sum_squares(piece, 0, 1)
                    close()
                    sum_squares(piece, 1, 4)
                    full.append(piece)
            close()
        for piece in waiting:
            add_and_store(piece, nc.vector)
